import numpy as np
import ml_dtypes


def mxq(x, axis, fmt="e4m3"):
    dtype, down = {"e4m3": (ml_dtypes.float8_e4m3fn, 7), "e5m2": (ml_dtypes.float8_e5m2, 14)}[fmt]
    v = np.moveaxis(np.asarray(x, np.float32).astype(ml_dtypes.bfloat16).astype(np.float64), axis, -1)
    blocks = v.reshape(v.shape[:-1] + (-1, 32))
    amax = np.abs(blocks).max(-1, keepdims=True)
    byte = np.maximum(np.where(amax > 0, np.frexp(amax)[1] - 1 + 127, 0) - down, 1)
    scale = np.exp2(byte - 127.0)
    codes = (blocks / scale).astype(np.float32).astype(dtype).astype(np.float64)
    return np.moveaxis((codes * scale).reshape(v.shape), -1, axis)


WIDE = False


def mx_kscale(k):
    if not WIDE:
        return np.ones(k)
    levels = np.array([10, -10, 5, -5, 0])
    if k % 512:
        return np.exp2(np.random.permutation(np.resize(levels, k // 32))).repeat(32)
    a = np.empty((k // 512, 16))
    for p in range(k // 512):
        a[p, :8] = np.random.permutation(np.resize(levels, 8))
        for g in range(8):
            far = levels[np.abs(levels - a[p, g]) >= 10]
            a[p, g + 8] = far[np.random.randint(len(far))]
    return np.exp2(a.ravel()).repeat(32)


BF16 = ml_dtypes.bfloat16


def bf(x):
    return np.asarray(x, np.float32).astype(BF16)


def f64(x):
    return np.asarray(x).astype(np.float64)


B, S, DIM, HEADS, DH = 1, 128, 512, 4, 128
HD = HEADS * DH
LN_EPS = 1e-5


def setup_inputs():
    s, t = mx_kscale(DIM), mx_kscale(HD)
    return {
        "x": bf(np.random.standard_normal((S, DIM)) + 0.5),
        "ln_w": bf((1.0 + 0.1 * np.random.standard_normal(DIM)) * s),
        "ln_b": bf(0.1 * np.random.standard_normal(DIM) * s),
        "W_c": bf(np.random.standard_normal((HD, DIM)) / np.sqrt(DIM) / s * t[:, None]),
        "b_c": bf(0.1 * np.random.standard_normal(HD) * t),
        "W_K": bf(np.random.standard_normal((HEADS, DH, DH, DH)) * 0.5 / np.sqrt(HD) / t.reshape(HEADS, 1, 1, DH)),
    }


def reference(x, ln_w, ln_b, W_c, b_c, W_K):
    x = f64(x)
    mu = x.mean(-1, keepdims=True)
    var = x.var(-1, keepdims=True)
    xn = (x - mu) / np.sqrt(var + LN_EPS) * f64(ln_w) + f64(ln_b)
    c = (mxq(xn, 1, "e4m3") @ mxq(f64(W_c), 1, "e4m3").T) + f64(b_c)
    wk = f64(W_K).transpose(0, 3, 1, 2).reshape(HD, DH * DH)
    return (mxq(c, 1, "e4m3") @ mxq(wk, 0, "e4m3")).reshape(S, DH, DH)

@@ -1,0 +1,318 @@
+from contextlib import ExitStack
+
+import concourse.mybir as mybir
+from concourse.masks import make_identity
+
+F32 = mybir.dt.float32
+BF16 = mybir.dt.bfloat16
+U32 = mybir.dt.uint32
+U8 = mybir.dt.uint8
+FP8X4 = mybir.dt.float8_e4m3fn_x4
+ALU = mybir.AluOpType
+ACTF = mybir.ActivationFunctionType
+
+P = 128
+DIM = 512
+ROWS = 128 * 128
+LN_EPS = 1e-5
+FLOPS = 2 * 128 * 512 * 512 + 2 * 128 * 512 * ROWS
+
+S1_DT = F32
+
+CHUNK_ROWS = [4, 4, 8, 8, 16, 16, 16, 16, 16, 8, 8, 4, 4]
+RAW_BUFS = {4: 2, 8: 2, 16: 3}
+STAGE_BUFS = {4: 2, 8: 2, 16: 5}
+FIRST_LOADS = 7
+V_SHARE_FROM = 6
+
+
+def tile_trittentioncube_pa_kernel(tc, x, ln_w, ln_b, W_c, b_c, W_K, out):
+    nc = tc.nc
+    wk = W_K.rearrange("n i j k -> n (i j) k")
+    out2 = out.rearrange("r i j -> r (i j)")
+
+    chunks = []
+    units = []
+    row0 = 0
+    for g, C in enumerate(CHUNK_ROWS):
+        U = min(C, 8)
+        mine = []
+        for c0 in range(0, C, U):
+            mine.append(len(units))
+            units.append({"g": g, "C": C, "U": U, "c0": c0})
+        chunks.append({"C": C, "row0": row0, "units": mine})
+        row0 += P * C
+    assert row0 == ROWS
+    NU = len(units)
+    NG = len(chunks)
+
+    with ExitStack() as ctx:
+        keep = ctx.enter_context(tc.tile_pool(name="keep", bufs=1))
+        rawp = ctx.enter_context(tc.tile_pool(name="rawp", bufs=2))
+        work = ctx.enter_context(tc.tile_pool(name="work", bufs=3))
+        stp = ctx.enter_context(tc.tile_pool(name="stp", bufs=2))
+        psum = ctx.enter_context(tc.psum_pool(name="psum", bufs=4))
+        ctx.enter_context(tc.manual_schedule())
+
+        raw_t = {}
+        R_t = {}
+        xt_t = {}
+        grp_t = {}
+        code_t = {}
+        scale_t = {}
+        mm_t = {}
+        stage_t = {}
+        state = {"next_load": 0, "held": []}
+        slot_hist = {4: [], 8: [], 16: []}
+
+        def load(g):
+            C = chunks[g]["C"]
+            r0 = chunks[g]["row0"]
+            raw = rawp.tile([P, 4, C * 128], BF16, name="raw%d" % C, tag="raw%d" % C, bufs=RAW_BUFS[C])
+            nc.sync.dma_start(
+                out=raw[:],
+                in_=wk[:, r0 : r0 + P * C, :].rearrange("n (p c) k -> p n (c k)", c=C),
+            )
+            raw_t[g] = raw
+            slot_hist[C].append(g)
+            state["next_load"] = g + 1
+
+        def more_loads(j):
+            while state["next_load"] < NG:
+                g = state["next_load"]
+                C = chunks[g]["C"]
+                h = slot_hist[C]
+                if len(h) >= RAW_BUFS[C]:
+                    old = h[len(h) - RAW_BUFS[C]]
+                    if chunks[old]["units"][-1] > j:
+                        break
+                load(g)
+
+        def reorder(j):
+            u_ = units[j]
+            U = u_["U"]
+            c0 = u_["c0"]
+            rw = raw_t[u_["g"]][:].bitcast(F32).rearrange("p n (c q u) -> p u c n q", q=32, u=2)
+            Rt = work.tile([P, U, 2, 128], F32, name="Rt", tag="Rt", bufs=3)
+            Rv = Rt[:].rearrange("p c u (n q) -> p u c n q", n=4)
+            for u in range(2):
+                nc.vector.tensor_copy(out=Rv[:, u], in_=rw[:, u, c0 : c0 + U])
+            R_t[j] = Rt
+            more_loads(j)
+
+        def transposes(j):
+            U = units[j]["U"]
+            Rt = R_t[j]
+            xt_t[j] = []
+            for b in range(U // 2):
+                xt = psum.tile([P, 4, 128], F32, name="xt", tag="tp", bufs=4)
+                for cl in range(2):
+                    for u in range(2):
+                        nc.tensor.transpose(xt[:, 2 * cl + u, :], Rt[:, 2 * b + cl, u, :], ident[:])
+                xt_t[j].append(xt)
+
+        def v_banks(j):
+            return 1 if j >= V_SHARE_FROM else 0
+
+        def copy_bank(j, b, eng):
+            gw = grp_t[j][:].bitcast(F32)
+            dst = gw[:, 512 * b : 512 * (b + 1)].rearrange("q (c p u) -> q c p u", c=2, u=2)
+            src = xt_t[j][b][:].rearrange("q (c u) p -> q c p u", u=2)
+            if eng == "S":
+                nc.scalar.copy(out=dst, in_=src)
+            else:
+                nc.vector.tensor_copy(out=dst, in_=src)
+
+        def copies_s(j):
+            U = units[j]["U"]
+            grp_t[j] = work.tile([P, U * 512], BF16, name="grp", tag="grp", bufs=3, align_bytes=64)
+            for b in range(U // 2 - v_banks(j)):
+                copy_bank(j, b, "S")
+
+        def copies_v(j):
+            U = units[j]["U"]
+            for b in range(U // 2 - v_banks(j), U // 2):
+                copy_bank(j, b, "V")
+
+        def quantize(j):
+            U = units[j]["U"]
+            codes = work.tile([P, U * 128], U32, name="codes", tag="codes", bufs=4, align_bytes=64)
+            scales = work.tile([P, U * 128], U8, name="scales", tag="scales", bufs=4, align_bytes=64)
+            nc.vector.quantize_mx(out=codes[:].bitcast(FP8X4), scales=scales[:], in_=grp_t[j][:])
+            code_t[j] = codes
+            scale_t[j] = scales
+
+        def multiply(j):
+            U = units[j]["U"]
+            mm_t[j] = []
+            for h in range(U // 4):
+                mm = psum.tile([P, 512], F32, name="mm", tag="mm", bufs=4)
+                cols = slice(512 * h, 512 * (h + 1))
+                nc.tensor.matmul_mx(
+                    out=mm[:],
+                    lhsT=c_codes[:].bitcast(FP8X4),
+                    lhsT_scale=c_scales[:],
+                    rhs=code_t[j][:, cols].bitcast(FP8X4),
+                    rhs_scale=scale_t[j][:, cols],
+                    start=True,
+                    stop=True,
+                )
+                mm_t[j].append(mm)
+
+        def store(g):
+            C = chunks[g]["C"]
+            r0 = chunks[g]["row0"]
+            nc.sync.dma_start(out=out2[:, r0 : r0 + P * C], in_=stage_t[g][:])
+
+        def out_copies(j):
+            u_ = units[j]
+            g = u_["g"]
+            C = u_["C"]
+            if u_["c0"] == 0:
+                stage_t[g] = stp.tile([P, P * C], F32, name="stage%d" % C, tag="stage%d" % C, bufs=STAGE_BUFS[C], align_bytes=64)
+            sv = stage_t[g][:].rearrange("r (p c) -> r p c", c=C)
+            for h in range(u_["U"] // 4):
+                cc = u_["c0"] + 4 * h
+                nc.scalar.copy(out=sv[:, :, cc : cc + 4], in_=mm_t[j][h][:].rearrange("r (c p) -> r p c", c=4))
+            if chunks[g]["units"][-1] == j:
+                state["held"].append(g)
+                if state["next_load"] >= NG:
+                    for gg in state["held"]:
+                        store(gg)
+                    state["held"] = []
+
+        x_sb = keep.tile([P, DIM], BF16, name="x_sb")
+        nc.sync.dma_start(out=x_sb[:], in_=x)
+        lnw = keep.tile([P, 4], BF16, name="lnw")
+        lnb = keep.tile([P, 4], BF16, name="lnb")
+        bc = keep.tile([P, 4], BF16, name="bc")
+        nc.scalar.dma_start(out=lnw[:], in_=ln_w.rearrange("(p t) -> p t", t=4))
+        nc.scalar.dma_start(out=lnb[:], in_=ln_b.rearrange("(p t) -> p t", t=4))
+        nc.scalar.dma_start(out=bc[:], in_=b_c.rearrange("(p t) -> p t", t=4))
+        load(0)
+        wc_raw = keep.tile([P, 4, DIM], BF16, name="wc_raw")
+        nc.sync.dma_start(out=wc_raw[:], in_=W_c.rearrange("(m t) d -> m t d", t=4))
+        for g in range(1, FIRST_LOADS):
+            load(g)
+
+        ident = keep.tile([P, P], F32, name="ident")
+        make_identity(nc, ident[:])
+        one = keep.tile([P, 1], F32, name="one")
+        nc.vector.memset(one[:], 1.0)
+        warm = keep.tile([P, 1], F32, name="warm")
+        nc.scalar.activation(out=warm[:], in_=one[:], func=ACTF.Sqrt)
+
+        stats = keep.tile([P, 6], F32, name="stats")
+        nc.vector.bn_stats(out=stats[:], in_=x_sb[:])
+        mv = keep.tile([P, 2], F32, name="mv")
+        nc.vector.bn_aggr(out=mv[:], in_=stats[:])
+        std = keep.tile([P, 1], F32, name="std")
+        nc.scalar.activation(out=std[:], in_=mv[:, 1:2], func=ACTF.Sqrt, bias=LN_EPS, scale=1.0)
+        rstd = keep.tile([P, 1], F32, name="rstd")
+        nc.vector.reciprocal(out=rstd[:], in_=std[:])
+        xhat = keep.tile([P, 4, 128], F32, name="xhat")
+        nc.vector.tensor_scalar(
+            out=xhat[:],
+            in0=x_sb[:].rearrange("r (q t) -> r t q", t=4),
+            scalar1=mv[:, 0:1],
+            scalar2=rstd[:],
+            op0=ALU.subtract,
+            op1=ALU.mult,
+        )
+        xT = psum.tile([P, 4, 128], F32, name="xT", tag="tp", bufs=4)
+        for t in range(4):
+            nc.tensor.transpose(xT[:, t, :], xhat[:, t, :], ident[:])
+        reorder(0)
+        xw = keep.tile([P, 128, 4], F32, name="xw")
+        nc.vector.tensor_tensor(
+            out=xw[:],
+            in0=xT[:].rearrange("q t r -> q r t"),
+            in1=lnw[:].rearrange("p (o t) -> p o t", o=1).to_broadcast([P, 128, 4]),
+            op=ALU.mult,
+        )
+        xg = keep.tile([P, 128, 4], BF16, name="xg", align_bytes=64)
+        nc.vector.tensor_tensor(
+            out=xg[:],
+            in0=xw[:],
+            in1=lnb[:].rearrange("p (o t) -> p o t", o=1).to_broadcast([P, 128, 4]),
+            op=ALU.add,
+        )
+
+        wcw = wc_raw[:].bitcast(F32)
+        wc_grp = keep.tile([P, 4 * DIM], BF16, name="wc_grp", align_bytes=64)
+        wc_gw = wc_grp[:].bitcast(F32)
+        wts = []
+        for b in range(2):
+            wt = psum.tile([P, 4, 128], F32, name="wt", tag="tp", bufs=4)
+            for tl in range(2):
+                for u in range(2):
+                    nc.tensor.transpose(wt[:, 2 * tl + u, :], wcw[:, 2 * b + tl, u:256:2], ident[:])
+            wts.append(wt)
+        for b in range(2):
+            nc.scalar.copy(
+                out=wc_gw[:, 512 * b : 512 * (b + 1)].rearrange("q (t m u) -> q t m u", t=2, u=2),
+                in_=wts[b][:].rearrange("q (t u) m -> q t m u", u=2),
+            )
+
+        transposes(0)
+        copies_s(0)
+        reorder(1)
+        x_codes = keep.tile([P, 128], U32, name="x_codes", align_bytes=64)
+        x_scales = keep.tile([P, 128], U8, name="x_scales", align_bytes=64)
+        nc.vector.quantize_mx(out=x_codes[:].bitcast(FP8X4), scales=x_scales[:], in_=xg[:].rearrange("q r t -> q (r t)"))
+        transposes(1)
+        copies_s(1)
+        wc_codes = keep.tile([P, DIM], U32, name="wc_codes", align_bytes=64)
+        wc_scales = keep.tile([P, DIM], U8, name="wc_scales", align_bytes=64)
+        nc.vector.quantize_mx(out=wc_codes[:].bitcast(FP8X4), scales=wc_scales[:], in_=wc_grp[:])
+
+        s1 = psum.tile([P, 4, 128], S1_DT, name="s1", tag="mm", bufs=4)
+        for t in range(4):
+            cols = slice(128 * t, 128 * (t + 1))
+            nc.tensor.matmul_mx(
+                out=s1[:, t, :],
+                lhsT=wc_codes[:, cols].bitcast(FP8X4),
+                lhsT_scale=wc_scales[:, cols],
+                rhs=x_codes[:].bitcast(FP8X4),
+                rhs_scale=x_scales[:],
+                start=True,
+                stop=True,
+            )
+        reorder(2)
+        transposes(2)
+        copies_s(2)
+        quantize(0)
+        cg = keep.tile([P, 128, 4], BF16, name="cg", align_bytes=64)
+        nc.vector.tensor_tensor(
+            out=cg[:],
+            in0=s1[:].rearrange("m t r -> m r t"),
+            in1=bc[:].rearrange("p (o t) -> p o t", o=1).to_broadcast([P, 128, 4]),
+            op=ALU.add,
+        )
+        quantize(1)
+        c_codes = keep.tile([P, 128], U32, name="c_codes", align_bytes=64)
+        c_scales = keep.tile([P, 128], U8, name="c_scales", align_bytes=64)
+        nc.vector.quantize_mx(out=c_codes[:].bitcast(FP8X4), scales=c_scales[:], in_=cg[:].rearrange("m r t -> m (r t)"))
+        reorder(3)
+        transposes(3)
+        copies_s(3)
+        multiply(0)
+        multiply(1)
+        quantize(2)
+        multiply(2)
+        out_copies(0)
+        out_copies(1)
+
+        for s in range(4, NU + 4):
+            if 3 <= s - 3 < NU:
+                quantize(s - 3)
+            if 4 <= s - 2 < NU:
+                transposes(s - 2)
+                copies_s(s - 2)
+                copies_v(s - 2)
+            if s < NU:
+                reorder(s)
+            if 3 <= s - 3 < NU:
+                multiply(s - 3)
+            if 2 <= s - 4 < NU:
+                out_copies(s - 4)

@@ -24,6 +24,8 @@ RAW_BUFS = {4: 2, 8: 2, 16: 3}
 STAGE_BUFS = {4: 2, 8: 2, 16: 5}
 FIRST_LOADS = 7
 V_SHARE_FROM = 6
+MM_TIMES = 2
+V_OUT_LAST = 2
 
 
 def tile_trittentioncube_pa_kernel(tc, x, ln_w, ln_b, W_c, b_c, W_K, out):
@@ -92,19 +94,26 @@ def tile_trittentioncube_pa_kernel(tc, x, ln_w, ln_b, W_c, b_c, W_K, out):
             u_ = units[j]
             U = u_["U"]
             c0 = u_["c0"]
-            rw = raw_t[u_["g"]][:].bitcast(F32).rearrange("p n (c q u) -> p u c n q", q=32, u=2)
+            rw = raw_t[u_["g"]][:].bitcast(F32).rearrange("p n (c q u) -> p c u n q", q=32, u=2)
             Rt = work.tile([P, U, 2, 128], F32, name="Rt", tag="Rt", bufs=3)
-            Rv = Rt[:].rearrange("p c u (n q) -> p u c n q", n=4)
-            for u in range(2):
-                nc.vector.tensor_copy(out=Rv[:, u], in_=rw[:, u, c0 : c0 + U])
+            Rv = Rt[:].rearrange("p c u (n q) -> p c u n q", n=4)
+            nc.vector.tensor_copy(out=Rv, in_=rw[:, c0 : c0 + U])
             R_t[j] = Rt
             more_loads(j)
 
-        def transposes(j):
-            U = units[j]["U"]
+        def half_banks(j, half):
+            nb = units[j]["U"] // 2
+            if half is None:
+                return list(range(nb))
+            if nb == 2:
+                return [0, 1] if half == 0 else []
+            return [2 * half, 2 * half + 1]
+
+        def transposes(j, half=None):
             Rt = R_t[j]
-            xt_t[j] = []
-            for b in range(U // 2):
+            if j not in xt_t:
+                xt_t[j] = []
+            for b in half_banks(j, half):
                 xt = psum.tile([P, 4, 128], F32, name="xt", tag="tp", bufs=4)
                 for cl in range(2):
                     for u in range(2):
@@ -123,11 +132,13 @@ def tile_trittentioncube_pa_kernel(tc, x, ln_w, ln_b, W_c, b_c, W_K, out):
             else:
                 nc.vector.tensor_copy(out=dst, in_=src)
 
-        def copies_s(j):
+        def copies_s(j, half=None):
             U = units[j]["U"]
-            grp_t[j] = work.tile([P, U * 512], BF16, name="grp", tag="grp", bufs=3, align_bytes=64)
-            for b in range(U // 2 - v_banks(j)):
-                copy_bank(j, b, "S")
+            if j not in grp_t:
+                grp_t[j] = work.tile([P, U * 512], BF16, name="grp", tag="grp", bufs=3, align_bytes=64)
+            for b in half_banks(j, half):
+                if b < U // 2 - v_banks(j):
+                    copy_bank(j, b, "S")
 
         def copies_v(j):
             U = units[j]["U"]
@@ -142,21 +153,25 @@ def tile_trittentioncube_pa_kernel(tc, x, ln_w, ln_b, W_c, b_c, W_K, out):
             code_t[j] = codes
             scale_t[j] = scales
 
-        def multiply(j):
+        def multiply(j, half=None):
             U = units[j]["U"]
-            mm_t[j] = []
+            if j not in mm_t:
+                mm_t[j] = []
             for h in range(U // 4):
+                if half is not None and h != half:
+                    continue
                 mm = psum.tile([P, 512], F32, name="mm", tag="mm", bufs=4)
                 cols = slice(512 * h, 512 * (h + 1))
-                nc.tensor.matmul_mx(
-                    out=mm[:],
-                    lhsT=c_codes[:].bitcast(FP8X4),
-                    lhsT_scale=c_scales[:],
-                    rhs=code_t[j][:, cols].bitcast(FP8X4),
-                    rhs_scale=scale_t[j][:, cols],
-                    start=True,
-                    stop=True,
-                )
+                for rep in range(MM_TIMES):
+                    nc.tensor.matmul_mx(
+                        out=mm[:],
+                        lhsT=c_codes[:].bitcast(FP8X4),
+                        lhsT_scale=c_scales[:],
+                        rhs=code_t[j][:, cols].bitcast(FP8X4),
+                        rhs_scale=scale_t[j][:, cols],
+                        start=True,
+                        stop=True,
+                    )
                 mm_t[j].append(mm)
 
         def store(g):
@@ -173,7 +188,11 @@ def tile_trittentioncube_pa_kernel(tc, x, ln_w, ln_b, W_c, b_c, W_K, out):
             sv = stage_t[g][:].rearrange("r (p c) -> r p c", c=C)
             for h in range(u_["U"] // 4):
                 cc = u_["c0"] + 4 * h
-                nc.scalar.copy(out=sv[:, :, cc : cc + 4], in_=mm_t[j][h][:].rearrange("r (c p) -> r p c", c=4))
+                src = mm_t[j][h][:].rearrange("r (c p) -> r p c", c=4)
+                if j >= NU - V_OUT_LAST:
+                    nc.vector.tensor_copy(out=sv[:, :, cc : cc + 4], in_=src)
+                else:
+                    nc.scalar.copy(out=sv[:, :, cc : cc + 4], in_=src)
             if chunks[g]["units"][-1] == j:
                 state["held"].append(g)
                 if state["next_load"] >= NG:
@@ -303,16 +322,21 @@ def tile_trittentioncube_pa_kernel(tc, x, ln_w, ln_b, W_c, b_c, W_K, out):
         out_copies(0)
         out_copies(1)
 
-        for s in range(4, NU + 4):
+        for s in range(4, NU + 5):
             if 3 <= s - 3 < NU:
                 quantize(s - 3)
             if 4 <= s - 2 < NU:
-                transposes(s - 2)
-                copies_s(s - 2)
+                transposes(s - 2, 0)
+                copies_s(s - 2, 0)
+            if 3 <= s - 4 < NU:
+                multiply(s - 4, 0)
+            if 4 <= s - 2 < NU:
+                transposes(s - 2, 1)
+                copies_s(s - 2, 1)
                 copies_v(s - 2)
+            if 3 <= s - 4 < NU:
+                multiply(s - 4, 1)
             if s < NU:
                 reorder(s)
-            if 3 <= s - 3 < NU:
-                multiply(s - 3)
-            if 2 <= s - 4 < NU:
-                out_copies(s - 4)
+            if 2 <= s - 5 < NU:
+                out_copies(s - 5)

@@ -26,6 +26,9 @@ FIRST_LOADS = 7
 V_SHARE_FROM = 6
 MM_TIMES = 2
 V_OUT_LAST = 2
+V_TWO_BANKS = (14, 15)
+WARM_FIRST = 6
+WARM_EACH = 2
 
 
 def tile_trittentioncube_pa_kernel(tc, x, ln_w, ln_b, W_c, b_c, W_K, out):
@@ -121,7 +124,13 @@ def tile_trittentioncube_pa_kernel(tc, x, ln_w, ln_b, W_c, b_c, W_K, out):
                 xt_t[j].append(xt)
 
         def v_banks(j):
+            if j in V_TWO_BANKS:
+                return 2
             return 1 if j >= V_SHARE_FROM else 0
+
+        def keep_warm(n):
+            for i in range(n):
+                nc.tensor.matmul(out=warm_ps[:], lhsT=ident[:], rhs=ident[:], start=True, stop=True)
 
         def copy_bank(j, b, eng):
             gw = grp_t[j][:].bitcast(F32)
@@ -216,6 +225,8 @@ def tile_trittentioncube_pa_kernel(tc, x, ln_w, ln_b, W_c, b_c, W_K, out):
 
         ident = keep.tile([P, P], F32, name="ident")
         make_identity(nc, ident[:])
+        warm_ps = psum.tile([P, P], F32, name="warm_ps", tag="mm", bufs=4)
+        keep_warm(WARM_FIRST)
         one = keep.tile([P, 1], F32, name="one")
         nc.vector.memset(one[:], 1.0)
         warm = keep.tile([P, 1], F32, name="warm")
@@ -241,6 +252,7 @@ def tile_trittentioncube_pa_kernel(tc, x, ln_w, ln_b, W_c, b_c, W_K, out):
         xT = psum.tile([P, 4, 128], F32, name="xT", tag="tp", bufs=4)
         for t in range(4):
             nc.tensor.transpose(xT[:, t, :], xhat[:, t, :], ident[:])
+        keep_warm(WARM_EACH)
         reorder(0)
         xw = keep.tile([P, 128, 4], F32, name="xw")
         nc.vector.tensor_tensor(
@@ -273,12 +285,14 @@ def tile_trittentioncube_pa_kernel(tc, x, ln_w, ln_b, W_c, b_c, W_K, out):
                 in_=wts[b][:].rearrange("q (t u) m -> q t m u", u=2),
             )
 
+        keep_warm(WARM_EACH)
         transposes(0)
         copies_s(0)
         reorder(1)
         x_codes = keep.tile([P, 128], U32, name="x_codes", align_bytes=64)
         x_scales = keep.tile([P, 128], U8, name="x_scales", align_bytes=64)
         nc.vector.quantize_mx(out=x_codes[:].bitcast(FP8X4), scales=x_scales[:], in_=xg[:].rearrange("q r t -> q (r t)"))
+        keep_warm(WARM_EACH)
         transposes(1)
         copies_s(1)
         wc_codes = keep.tile([P, DIM], U32, name="wc_codes", align_bytes=64)
@@ -298,6 +312,7 @@ def tile_trittentioncube_pa_kernel(tc, x, ln_w, ln_b, W_c, b_c, W_K, out):
                 stop=True,
             )
         reorder(2)
+        keep_warm(WARM_EACH)
         transposes(2)
         copies_s(2)
         quantize(0)
@@ -313,6 +328,7 @@ def tile_trittentioncube_pa_kernel(tc, x, ln_w, ln_b, W_c, b_c, W_K, out):
         c_scales = keep.tile([P, 128], U8, name="c_scales", align_bytes=64)
         nc.vector.quantize_mx(out=c_codes[:].bitcast(FP8X4), scales=c_scales[:], in_=cg[:].rearrange("m r t -> m (r t)"))
         reorder(3)
+        keep_warm(WARM_EACH)
         transposes(3)
         copies_s(3)
         multiply(0)

from contextlib import ExitStack

import concourse.mybir as mybir
from concourse.masks import make_identity

F32 = mybir.dt.float32
BF16 = mybir.dt.bfloat16
U32 = mybir.dt.uint32
U8 = mybir.dt.uint8
FP8X4 = mybir.dt.float8_e4m3fn_x4
ALU = mybir.AluOpType
ACTF = mybir.ActivationFunctionType

P = 128
DIM = 512
ROWS = 128 * 128
LN_EPS = 1e-5
FLOPS = 2 * 128 * 512 * 512 + 2 * 128 * 512 * ROWS

S1_DT = F32

CHUNK_ROWS = [4, 4, 8, 8, 16, 16, 16, 16, 16, 8, 8, 4, 4]
RAW_BUFS = {4: 2, 8: 2, 16: 3}
STAGE_BUFS = {4: 2, 8: 2, 16: 5}
FIRST_LOADS = 7
V_SHARE_FROM = 6
MM_TIMES = 2
V_OUT_LAST = 2
V_TWO_BANKS = (14, 15)
WARM_FIRST = 6
WARM_EACH = 2


def tile_trittentioncube_pa_kernel(tc, x, ln_w, ln_b, W_c, b_c, W_K, out):
    nc = tc.nc
    wk = W_K.rearrange("n i j k -> n (i j) k")
    out2 = out.rearrange("r i j -> r (i j)")

    chunks = []
    units = []
    row0 = 0
    for g, C in enumerate(CHUNK_ROWS):
        U = min(C, 8)
        mine = []
        for c0 in range(0, C, U):
            mine.append(len(units))
            units.append({"g": g, "C": C, "U": U, "c0": c0})
        chunks.append({"C": C, "row0": row0, "units": mine})
        row0 += P * C
    assert row0 == ROWS
    NU = len(units)
    NG = len(chunks)

    with ExitStack() as ctx:
        keep = ctx.enter_context(tc.tile_pool(name="keep", bufs=1))
        rawp = ctx.enter_context(tc.tile_pool(name="rawp", bufs=2))
        work = ctx.enter_context(tc.tile_pool(name="work", bufs=3))
        stp = ctx.enter_context(tc.tile_pool(name="stp", bufs=2))
        psum = ctx.enter_context(tc.psum_pool(name="psum", bufs=4))
        ctx.enter_context(tc.manual_schedule())

        raw_t = {}
        R_t = {}
        xt_t = {}
        grp_t = {}
        code_t = {}
        scale_t = {}
        mm_t = {}
        stage_t = {}
        state = {"next_load": 0, "held": []}
        slot_hist = {4: [], 8: [], 16: []}

        def load(g):
            C = chunks[g]["C"]
            r0 = chunks[g]["row0"]
            raw = rawp.tile([P, 4, C * 128], BF16, name="raw%d" % C, tag="raw%d" % C, bufs=RAW_BUFS[C])
            nc.sync.dma_start(
                out=raw[:],
                in_=wk[:, r0 : r0 + P * C, :].rearrange("n (p c) k -> p n (c k)", c=C),
            )
            raw_t[g] = raw
            slot_hist[C].append(g)
            state["next_load"] = g + 1

        def more_loads(j):
            while state["next_load"] < NG:
                g = state["next_load"]
                C = chunks[g]["C"]
                h = slot_hist[C]
                if len(h) >= RAW_BUFS[C]:
                    old = h[len(h) - RAW_BUFS[C]]
                    if chunks[old]["units"][-1] > j:
                        break
                load(g)

        def reorder(j):
            u_ = units[j]
            U = u_["U"]
            c0 = u_["c0"]
            rw = raw_t[u_["g"]][:].bitcast(F32).rearrange("p n (c q u) -> p c u n q", q=32, u=2)
            Rt = work.tile([P, U, 2, 128], F32, name="Rt", tag="Rt", bufs=3)
            Rv = Rt[:].rearrange("p c u (n q) -> p c u n q", n=4)
            nc.vector.tensor_copy(out=Rv, in_=rw[:, c0 : c0 + U])
            R_t[j] = Rt
            more_loads(j)

        def half_banks(j, half):
            nb = units[j]["U"] // 2
            if half is None:
                return list(range(nb))
            if nb == 2:
                return [0, 1] if half == 0 else []
            return [2 * half, 2 * half + 1]

        def transposes(j, half=None):
            Rt = R_t[j]
            if j not in xt_t:
                xt_t[j] = []
            for b in half_banks(j, half):
                xt = psum.tile([P, 4, 128], F32, name="xt", tag="tp", bufs=4)
                for cl in range(2):
                    for u in range(2):
                        nc.tensor.transpose(xt[:, 2 * cl + u, :], Rt[:, 2 * b + cl, u, :], ident[:])
                xt_t[j].append(xt)

        def v_banks(j):
            if j in V_TWO_BANKS:
                return 2
            return 1 if j >= V_SHARE_FROM else 0

        def keep_warm(n):
            for i in range(n):
                nc.tensor.matmul(out=warm_ps[:], lhsT=ident[:], rhs=ident[:], start=True, stop=True)

        def copy_bank(j, b, eng):
            gw = grp_t[j][:].bitcast(F32)
            dst = gw[:, 512 * b : 512 * (b + 1)].rearrange("q (c p u) -> q c p u", c=2, u=2)
            src = xt_t[j][b][:].rearrange("q (c u) p -> q c p u", u=2)
            if eng == "S":
                nc.scalar.copy(out=dst, in_=src)
            else:
                nc.vector.tensor_copy(out=dst, in_=src)

        def copies_s(j, half=None):
            U = units[j]["U"]
            if j not in grp_t:
                grp_t[j] = work.tile([P, U * 512], BF16, name="grp", tag="grp", bufs=3, align_bytes=64)
            for b in half_banks(j, half):
                if b < U // 2 - v_banks(j):
                    copy_bank(j, b, "S")

        def copies_v(j):
            U = units[j]["U"]
            for b in range(U // 2 - v_banks(j), U // 2):
                copy_bank(j, b, "V")

        def quantize(j):
            U = units[j]["U"]
            codes = work.tile([P, U * 128], U32, name="codes", tag="codes", bufs=4, align_bytes=64)
            scales = work.tile([P, U * 128], U8, name="scales", tag="scales", bufs=4, align_bytes=64)
            nc.vector.quantize_mx(out=codes[:].bitcast(FP8X4), scales=scales[:], in_=grp_t[j][:])
            code_t[j] = codes
            scale_t[j] = scales

        def multiply(j, half=None):
            U = units[j]["U"]
            if j not in mm_t:
                mm_t[j] = []
            for h in range(U // 4):
                if half is not None and h != half:
                    continue
                mm = psum.tile([P, 512], F32, name="mm", tag="mm", bufs=4)
                cols = slice(512 * h, 512 * (h + 1))
                for rep in range(MM_TIMES):
                    nc.tensor.matmul_mx(
                        out=mm[:],
                        lhsT=c_codes[:].bitcast(FP8X4),
                        lhsT_scale=c_scales[:],
                        rhs=code_t[j][:, cols].bitcast(FP8X4),
                        rhs_scale=scale_t[j][:, cols],
                        start=True,
                        stop=True,
                    )
                mm_t[j].append(mm)

        def store(g):
            C = chunks[g]["C"]
            r0 = chunks[g]["row0"]
            nc.sync.dma_start(out=out2[:, r0 : r0 + P * C], in_=stage_t[g][:])

        def out_copies(j):
            u_ = units[j]
            g = u_["g"]
            C = u_["C"]
            if u_["c0"] == 0:
                stage_t[g] = stp.tile([P, P * C], F32, name="stage%d" % C, tag="stage%d" % C, bufs=STAGE_BUFS[C], align_bytes=64)
            sv = stage_t[g][:].rearrange("r (p c) -> r p c", c=C)
            for h in range(u_["U"] // 4):
                cc = u_["c0"] + 4 * h
                src = mm_t[j][h][:].rearrange("r (c p) -> r p c", c=4)
                if j >= NU - V_OUT_LAST:
                    nc.vector.tensor_copy(out=sv[:, :, cc : cc + 4], in_=src)
                else:
                    nc.scalar.copy(out=sv[:, :, cc : cc + 4], in_=src)
            if chunks[g]["units"][-1] == j:
                state["held"].append(g)
                if state["next_load"] >= NG:
                    for gg in state["held"]:
                        store(gg)
                    state["held"] = []

        x_sb = keep.tile([P, DIM], BF16, name="x_sb")
        nc.sync.dma_start(out=x_sb[:], in_=x)
        lnw = keep.tile([P, 4], BF16, name="lnw")
        lnb = keep.tile([P, 4], BF16, name="lnb")
        bc = keep.tile([P, 4], BF16, name="bc")
        nc.scalar.dma_start(out=lnw[:], in_=ln_w.rearrange("(p t) -> p t", t=4))
        nc.scalar.dma_start(out=lnb[:], in_=ln_b.rearrange("(p t) -> p t", t=4))
        nc.scalar.dma_start(out=bc[:], in_=b_c.rearrange("(p t) -> p t", t=4))
        load(0)
        wc_raw = keep.tile([P, 4, DIM], BF16, name="wc_raw")
        nc.sync.dma_start(out=wc_raw[:], in_=W_c.rearrange("(m t) d -> m t d", t=4))
        for g in range(1, FIRST_LOADS):
            load(g)

        ident = keep.tile([P, P], F32, name="ident")
        make_identity(nc, ident[:])
        warm_ps = psum.tile([P, P], F32, name="warm_ps", tag="mm", bufs=4)
        keep_warm(WARM_FIRST)
        one = keep.tile([P, 1], F32, name="one")
        nc.vector.memset(one[:], 1.0)
        warm = keep.tile([P, 1], F32, name="warm")
        nc.scalar.activation(out=warm[:], in_=one[:], func=ACTF.Sqrt)

        stats = keep.tile([P, 6], F32, name="stats")
        nc.vector.bn_stats(out=stats[:], in_=x_sb[:])
        mv = keep.tile([P, 2], F32, name="mv")
        nc.vector.bn_aggr(out=mv[:], in_=stats[:])
        std = keep.tile([P, 1], F32, name="std")
        nc.scalar.activation(out=std[:], in_=mv[:, 1:2], func=ACTF.Sqrt, bias=LN_EPS, scale=1.0)
        rstd = keep.tile([P, 1], F32, name="rstd")
        nc.vector.reciprocal(out=rstd[:], in_=std[:])
        xhat = keep.tile([P, 4, 128], F32, name="xhat")
        nc.vector.tensor_scalar(
            out=xhat[:],
            in0=x_sb[:].rearrange("r (q t) -> r t q", t=4),
            scalar1=mv[:, 0:1],
            scalar2=rstd[:],
            op0=ALU.subtract,
            op1=ALU.mult,
        )
        xT = psum.tile([P, 4, 128], F32, name="xT", tag="tp", bufs=4)
        for t in range(4):
            nc.tensor.transpose(xT[:, t, :], xhat[:, t, :], ident[:])
        keep_warm(WARM_EACH)
        reorder(0)
        xw = keep.tile([P, 128, 4], F32, name="xw")
        nc.vector.tensor_tensor(
            out=xw[:],
            in0=xT[:].rearrange("q t r -> q r t"),
            in1=lnw[:].rearrange("p (o t) -> p o t", o=1).to_broadcast([P, 128, 4]),
            op=ALU.mult,
        )
        xg = keep.tile([P, 128, 4], BF16, name="xg", align_bytes=64)
        nc.vector.tensor_tensor(
            out=xg[:],
            in0=xw[:],
            in1=lnb[:].rearrange("p (o t) -> p o t", o=1).to_broadcast([P, 128, 4]),
            op=ALU.add,
        )

        wcw = wc_raw[:].bitcast(F32)
        wc_grp = keep.tile([P, 4 * DIM], BF16, name="wc_grp", align_bytes=64)
        wc_gw = wc_grp[:].bitcast(F32)
        wts = []
        for b in range(2):
            wt = psum.tile([P, 4, 128], F32, name="wt", tag="tp", bufs=4)
            for tl in range(2):
                for u in range(2):
                    nc.tensor.transpose(wt[:, 2 * tl + u, :], wcw[:, 2 * b + tl, u:256:2], ident[:])
            wts.append(wt)
        for b in range(2):
            nc.scalar.copy(
                out=wc_gw[:, 512 * b : 512 * (b + 1)].rearrange("q (t m u) -> q t m u", t=2, u=2),
                in_=wts[b][:].rearrange("q (t u) m -> q t m u", u=2),
            )

        keep_warm(WARM_EACH)
        transposes(0)
        copies_s(0)
        reorder(1)
        x_codes = keep.tile([P, 128], U32, name="x_codes", align_bytes=64)
        x_scales = keep.tile([P, 128], U8, name="x_scales", align_bytes=64)
        nc.vector.quantize_mx(out=x_codes[:].bitcast(FP8X4), scales=x_scales[:], in_=xg[:].rearrange("q r t -> q (r t)"))
        keep_warm(WARM_EACH)
        transposes(1)
        copies_s(1)
        wc_codes = keep.tile([P, DIM], U32, name="wc_codes", align_bytes=64)
        wc_scales = keep.tile([P, DIM], U8, name="wc_scales", align_bytes=64)
        nc.vector.quantize_mx(out=wc_codes[:].bitcast(FP8X4), scales=wc_scales[:], in_=wc_grp[:])

        s1 = psum.tile([P, 4, 128], S1_DT, name="s1", tag="mm", bufs=4)
        for t in range(4):
            cols = slice(128 * t, 128 * (t + 1))
            nc.tensor.matmul_mx(
                out=s1[:, t, :],
                lhsT=wc_codes[:, cols].bitcast(FP8X4),
                lhsT_scale=wc_scales[:, cols],
                rhs=x_codes[:].bitcast(FP8X4),
                rhs_scale=x_scales[:],
                start=True,
                stop=True,
            )
        reorder(2)
        keep_warm(WARM_EACH)
        transposes(2)
        copies_s(2)
        quantize(0)
        cg = keep.tile([P, 128, 4], BF16, name="cg", align_bytes=64)
        nc.vector.tensor_tensor(
            out=cg[:],
            in0=s1[:].rearrange("m t r -> m r t"),
            in1=bc[:].rearrange("p (o t) -> p o t", o=1).to_broadcast([P, 128, 4]),
            op=ALU.add,
        )
        quantize(1)
        c_codes = keep.tile([P, 128], U32, name="c_codes", align_bytes=64)
        c_scales = keep.tile([P, 128], U8, name="c_scales", align_bytes=64)
        nc.vector.quantize_mx(out=c_codes[:].bitcast(FP8X4), scales=c_scales[:], in_=cg[:].rearrange("m r t -> m (r t)"))
        reorder(3)
        keep_warm(WARM_EACH)
        transposes(3)
        copies_s(3)
        multiply(0)
        multiply(1)
        quantize(2)
        multiply(2)
        out_copies(0)
        out_copies(1)

        for s in range(4, NU + 5):
            if 3 <= s - 3 < NU:
                quantize(s - 3)
            if 4 <= s - 2 < NU:
                transposes(s - 2, 0)
                copies_s(s - 2, 0)
            if 3 <= s - 4 < NU:
                multiply(s - 4, 0)
            if 4 <= s - 2 < NU:
                transposes(s - 2, 1)
                copies_s(s - 2, 1)
                copies_v(s - 2)
            if 3 <= s - 4 < NU:
                multiply(s - 4, 1)
            if s < NU:
                reorder(s)
            if 2 <= s - 5 < NU:
                out_copies(s - 5)
